import numpy as np
import ml_dtypes


def mxq(x, axis, fmt="e4m3"):
    dtype, down = {"e4m3": (ml_dtypes.float8_e4m3fn, 7), "e5m2": (ml_dtypes.float8_e5m2, 14)}[fmt]
    v = np.moveaxis(np.asarray(x, np.float32).astype(ml_dtypes.bfloat16).astype(np.float64), axis, -1)
    blocks = v.reshape(v.shape[:-1] + (-1, 32))
    amax = np.abs(blocks).max(-1, keepdims=True)
    byte = np.maximum(np.where(amax > 0, np.frexp(amax)[1] - 1 + 127, 0) - down, 1)
    scale = np.exp2(byte - 127.0)
    codes = (blocks / scale).astype(np.float32).astype(dtype).astype(np.float64)
    return np.moveaxis((codes * scale).reshape(v.shape), -1, axis)


WIDE = False


def mx_kscale(k):
    if not WIDE:
        return np.ones(k)
    levels = np.array([10, -10, 5, -5, 0])
    a = np.random.permutation(np.resize(levels, k // 512 * 4)).reshape(k // 512, 4)
    idx = np.arange(k)
    return np.exp2(a[idx // 512, idx % 128 // 32])


BF16 = ml_dtypes.bfloat16


def bf(x):
    return np.asarray(x, np.float32).astype(BF16)


def f64(x):
    return np.asarray(x).astype(np.float64)


E2M1 = np.array([0.0, 0.5, 1.0, 1.5, 2.0, 3.0, 4.0, 6.0, -0.0, -0.5, -1.0, -1.5, -2.0, -3.0, -4.0, -6.0])


def pack_weight(w, fmt):
    k, n = w.shape
    w = f64(bf(w)).reshape(k // 32, 32, n)
    amax = np.abs(w).max(1)
    if fmt == "e4m3":
        byte = np.frexp(amax)[1] - 1 + 127 - 7
    else:
        mant, ex = np.frexp(amax / 6.0)
        byte = np.where(mant > 0.5, ex, ex - 1) + 127
    byte = np.clip(np.where(amax > 0, byte, 1), 1, 254)
    scaled = (w * np.exp2(127.0 - byte)[:, None, :]).reshape(k, n).astype(np.float32)
    by_word = np.ascontiguousarray(scaled.reshape(k // 512, 128, 4, n).transpose(0, 1, 3, 2))
    if fmt == "e4m3":
        words = by_word.astype(ml_dtypes.float8_e4m3fn).view(np.uint8)
    else:
        c = by_word.astype(ml_dtypes.float4_e2m1fn).view(np.uint8) & 0xF
        words = c[..., 0::2] | (c[..., 1::2] << 4)
    return np.ascontiguousarray(words), np.ascontiguousarray(byte.astype(np.uint8).reshape(k // 512, 16, n))


def unpack_weight(words, scales, fmt):
    g, p, n, _ = words.shape
    if fmt == "e4m3":
        vals = np.ascontiguousarray(words).view(ml_dtypes.float8_e4m3fn).astype(np.float64)
    else:
        nib = np.empty((g, p, n, 4), np.uint8)
        nib[..., 0::2] = words & 0xF
        nib[..., 1::2] = words >> 4
        vals = E2M1[nib]
    vals = vals * np.repeat(np.exp2(scales.astype(np.float64) - 127.0), 8, axis=1)[..., None]
    return vals.transpose(0, 1, 3, 2).reshape(g * 512, n)


B, T, C, H, D, R = 4, 1024, 1024, 4, 128, 512
EPS = 1e-6
THETA = 10000.0
FMT = "e4m3"


def rmsnorm(v, w):
    var = np.mean(v * v, axis=-1, keepdims=True)
    return v * (1.0 / np.sqrt(var + EPS)) * w


def rope(v, cos, sin):
    re, im = v[..., 0::2], v[..., 1::2]
    c, s = cos[None, :, None, :], sin[None, :, None, :]
    return np.stack([re * c - im * s, re * s + im * c], axis=-1).reshape(v.shape)


def setup_inputs():
    s, t = mx_kscale(C), mx_kscale(R)
    ang = np.outer(np.arange(T), 1.0 / THETA ** (np.arange(0, D, 2) / D))
    x = bf(np.random.standard_normal((B, T, C)) * s)
    down_words, down_scales = pack_weight((np.random.standard_normal((R, C)) / np.sqrt(C) / s[None, :] * t[:, None]).T, FMT)
    up_words, up_scales = pack_weight((np.random.standard_normal((2 * H * D, R)) / np.sqrt(R) / t[None, :]).T, FMT)
    return {"x": x,
            "w_kv_down_words": down_words, "w_kv_down_scales": down_scales,
            "w_kv_up_words": up_words, "w_kv_up_scales": up_scales,
            "k_norm_w": bf(1.0 + 0.1 * np.random.standard_normal(D)),
            "freqs_cos": bf(np.cos(ang)), "freqs_sin": bf(np.sin(ang))}


def reference(x, w_kv_down_words, w_kv_down_scales, w_kv_up_words, w_kv_up_scales, k_norm_w, freqs_cos, freqs_sin):
    latent = mxq(f64(x), 2, "e4m3") @ unpack_weight(w_kv_down_words, w_kv_down_scales, FMT)
    kv = (mxq(latent, 2, "e4m3") @ unpack_weight(w_kv_up_words, w_kv_up_scales, FMT)).reshape(B, T, 2, H, D)
    xk, xv = kv[:, :, 0], kv[:, :, 1]
    return rope(rmsnorm(xk, f64(k_norm_w)), f64(freqs_cos), f64(freqs_sin)), xv

@@ -1,0 +1,323 @@
+from contextlib import ExitStack
+
+import concourse.masks as masks
+import concourse.mybir as mybir
+
+F32 = mybir.dt.float32
+BF16 = mybir.dt.bfloat16
+I32 = mybir.dt.int32
+U32 = mybir.dt.uint32
+U8 = mybir.dt.uint8
+FP8X4 = mybir.dt.float8_e4m3fn_x4
+MULT = mybir.AluOpType.mult
+ADD = mybir.AluOpType.add
+SQUARE = mybir.ActivationFunctionType.Square
+SQRT = mybir.ActivationFunctionType.Sqrt
+
+P = 128
+PACK = 4
+TOKENS = 4 * 1024
+SEQ = 1024
+C = 1024
+R = 512
+H = 4
+D = 128
+PAIRS = D // 2
+EPS = 1e-6
+
+DOWN_PASSES = C // (P * PACK)
+GROUP_TILES = 4
+N_TILES = TOKENS // P
+N_GROUPS = N_TILES // GROUP_TILES
+SEQ_TILES = SEQ // P
+ADD_HEADS = 2
+
+FLOPS = 2 * TOKENS * (C * R + R * 2 * H * D)
+
+
+def tile_mla_pa_t_kernel(
+    tc,
+    x,
+    w_kv_down_words,
+    w_kv_down_scales,
+    w_kv_up_words,
+    w_kv_up_scales,
+    k_norm_w,
+    freqs_cos,
+    freqs_sin,
+    out_0,
+    out_1,
+):
+    nc = tc.nc
+
+    x_groups = x.flatten_outer_dims().rearrange("(g p s) c -> g p s c", p=P, s=GROUP_TILES)
+    k_groups = out_0.rearrange("b t h d -> (b t) (h d)").rearrange(
+        "(g p s) n -> g p s n", p=P, s=GROUP_TILES
+    )
+    v_groups = out_1.rearrange("b t h d -> (b t) (h d)").rearrange(
+        "(g p s) n -> g p s n", p=P, s=GROUP_TILES
+    )
+
+    with ExitStack() as ctx:
+        ctx.enter_context(tc.manual_schedule())
+        const = ctx.enter_context(tc.tile_pool(name="const", bufs=1))
+        work = ctx.enter_context(tc.tile_pool(name="work", bufs=2))
+        kept = ctx.enter_context(tc.tile_pool(name="kept", bufs=3))
+        outs = ctx.enter_context(tc.tile_pool(name="outs", bufs=6))
+        psum_xt = ctx.enter_context(tc.psum_pool(name="psum_xt", bufs=2))
+        psum_lat = ctx.enter_context(tc.psum_pool(name="psum_lat", bufs=1))
+        psum_latt = ctx.enter_context(tc.psum_pool(name="psum_latt", bufs=1))
+        psum_k = ctx.enter_context(tc.psum_pool(name="psum_k", bufs=2))
+        psum_v = ctx.enter_context(tc.psum_pool(name="psum_v", bufs=2))
+
+        planes = const.tile([P, DOWN_PASSES * R + 2 * H * D], U8, name="planes", align_bytes=64)
+        planes_i32 = planes[:].bitcast(I32)
+        nc.vector.memset(planes_i32, 0)
+        eps_col = const.tile([P, 1], F32, name="eps_col")
+        nc.vector.memset(eps_col[:], EPS)
+
+        ident_f32 = const.tile([P, P], F32, name="ident_f32")
+        masks.make_identity(nc, ident_f32[:])
+        ident_bf16 = const.tile([P, P], BF16, name="ident_bf16")
+        masks.make_identity(nc, ident_bf16[:])
+
+        cos_sb = const.tile([P, SEQ_TILES, PAIRS], BF16, name="cos_sb")
+        sin_sb = const.tile([P, SEQ_TILES, PAIRS], BF16, name="sin_sb")
+        gain = const.tile([P, PAIRS, 2], BF16, name="gain")
+        nc.scalar.dma_start(
+            out=gain[:].rearrange("p j e -> p (j e)"), in_=k_norm_w.partition_broadcast(P)
+        )
+        table_view = "(a p s) j -> p a s j"
+        nc.scalar.dma_start(
+            out=cos_sb[:].rearrange("p (a s) j -> p a s j", s=GROUP_TILES),
+            in_=freqs_cos.rearrange(table_view, p=P, s=GROUP_TILES),
+        )
+        nc.scalar.dma_start(
+            out=sin_sb[:].rearrange("p (a s) j -> p a s j", s=GROUP_TILES),
+            in_=freqs_sin.rearrange(table_view, p=P, s=GROUP_TILES),
+        )
+        warm = const.tile([P, 1], F32, name="warm")
+        nc.scalar.activation(out=warm[:], in_=eps_col[:], func=SQRT)
+
+        x_sb = [const.tile([P, GROUP_TILES, C], BF16, name="x%d" % g) for g in range(N_GROUPS)]
+        w_down = const.tile([P, DOWN_PASSES, R * PACK], U8, name="w_down", align_bytes=64)
+        w_up = const.tile([P, 2 * H * D * PACK], U8, name="w_up", align_bytes=64)
+
+        nc.sync.dma_start(out=x_sb[0][:, 0, :], in_=x_groups[0, :, 0, :])
+        down_scales_i32 = w_kv_down_scales.bitcast(I32)
+        for quad in range(4):
+            nc.sync.dma_start(
+                out=planes_i32[32 * quad : 32 * quad + 4, 0 : DOWN_PASSES * R // 4].rearrange(
+                    "r (g n) -> r g n", g=DOWN_PASSES
+                ),
+                in_=down_scales_i32[:, 4 * quad : 4 * quad + 4, :].rearrange("g r n -> r g n"),
+            )
+        nc.sync.dma_start(
+            out=w_down[:].bitcast(I32),
+            in_=w_kv_down_words.rearrange("g p n t -> g p (n t)")
+            .bitcast(I32)
+            .rearrange("g p n -> p g n"),
+        )
+        for s in range(1, GROUP_TILES):
+            nc.sync.dma_start(out=x_sb[0][:, s, :], in_=x_groups[0, :, s, :])
+        up_scales_i32 = w_kv_up_scales.bitcast(I32)
+        for quad in range(4):
+            nc.sync.dma_start(
+                out=planes_i32[32 * quad : 32 * quad + 4, DOWN_PASSES * R // 4 :],
+                in_=up_scales_i32[0, 4 * quad : 4 * quad + 4, :],
+            )
+        nc.sync.dma_start(
+            out=w_up[:].bitcast(I32),
+            in_=w_kv_up_words[0].rearrange("p n t -> p (n t)").bitcast(I32),
+        )
+        for g in range(1, N_GROUPS):
+            nc.sync.dma_start(out=x_sb[g][:], in_=x_groups[g])
+
+        gain_cross = const.tile([P, 2, PAIRS], F32, name="gain_cross")
+        nc.gpsimd.tensor_scalar(
+            out=gain_cross[:, 0, :], in0=gain[:, :, 1], scalar1=-1.0, scalar2=0.0, op0=MULT, op1=ADD
+        )
+        nc.gpsimd.tensor_copy(out=gain_cross[:, 1, :], in_=gain[:, :, 0])
+        table_same = const.tile([P, SEQ_TILES, PAIRS, 2], F32, name="table_same")
+        table_cross = const.tile([P, SEQ_TILES, 2, PAIRS], F32, name="table_cross")
+        for a in range(0, SEQ_TILES, GROUP_TILES):
+            tiles = slice(a, a + GROUP_TILES)
+            nc.gpsimd.tensor_tensor(
+                out=table_same[:, tiles],
+                in0=cos_sb[:, tiles, :].unsqueeze(3).to_broadcast([P, GROUP_TILES, PAIRS, 2]),
+                in1=gain[:].unsqueeze(1).to_broadcast([P, GROUP_TILES, PAIRS, 2]),
+                op=MULT,
+            )
+            nc.gpsimd.tensor_tensor(
+                out=table_cross[:, tiles],
+                in0=sin_sb[:, tiles, :].unsqueeze(2).to_broadcast([P, GROUP_TILES, 2, PAIRS]),
+                in1=gain_cross[:].unsqueeze(1).to_broadcast([P, GROUP_TILES, 2, PAIRS]),
+                op=MULT,
+            )
+
+        xt_psum, x_grouped, x_codes, x_scales = {}, {}, {}, {}
+        lat_psum, lat_sorted, latt_psum, lat_grouped, lat_codes, lat_scales = {}, {}, {}, {}, {}, {}
+        k_psum, v_psum, rms, same, cross = {}, {}, {}, {}, {}
+
+        def transpose_x(i):
+            words = x_sb[i // GROUP_TILES][:, i % GROUP_TILES, :].bitcast(F32)
+            xt_psum[i] = psum_xt.tile([P, DOWN_PASSES, 2, P], F32, name="xt")
+            for g in range(DOWN_PASSES):
+                for u in range(2):
+                    nc.tensor.transpose(
+                        xt_psum[i][:, g, u, :],
+                        words[:, 2 * P * g + u : 2 * P * (g + 1) : 2],
+                        ident_f32[:],
+                    )
+
+        def regroup_x(i):
+            x_grouped[i] = work.tile([P, DOWN_PASSES, P, PACK], BF16, name="xg", align_bytes=64)
+            nc.scalar.copy(
+                out=x_grouped[i][:].bitcast(F32),
+                in_=xt_psum[i][:].rearrange("p g u m -> p g m u"),
+            )
+
+        def quantise_x(i):
+            x_codes[i] = kept.tile([P, DOWN_PASSES * P], U32, name="xq", align_bytes=64)
+            x_scales[i] = kept.tile([P, DOWN_PASSES * P], U8, name="xs", align_bytes=64)
+            nc.vector.quantize_mx(
+                out=x_codes[i][:].bitcast(FP8X4),
+                scales=x_scales[i][:],
+                in_=x_grouped[i][:].rearrange("p g m t -> p (g m t)"),
+            )
+
+        def down_matmul(i):
+            lat_psum[i] = psum_lat.tile([P, R], F32, name="lat")
+            for g in range(DOWN_PASSES):
+                tokens = slice(g * P, (g + 1) * P)
+                nc.tensor.matmul_mx(
+                    out=lat_psum[i][:],
+                    lhsT=x_codes[i][:, tokens].bitcast(FP8X4),
+                    lhsT_scale=x_scales[i][:, tokens],
+                    rhs=w_down[:, g, :].bitcast(FP8X4),
+                    rhs_scale=planes[:, g * R : (g + 1) * R],
+                    start=(g == 0),
+                    stop=(g == DOWN_PASSES - 1),
+                )
+
+        def round_latent(i):
+            lat_sorted[i] = work.tile([P, PACK, P], BF16, name="ls")
+            nc.scalar.copy(
+                out=lat_sorted[i][:], in_=lat_psum[i][:].rearrange("m (p t) -> m t p", t=PACK)
+            )
+
+        def transpose_latent(i):
+            latt_psum[i] = psum_latt.tile([P, PACK, P], BF16, name="latt")
+            for t in range(PACK):
+                nc.tensor.transpose(latt_psum[i][:, t, :], lat_sorted[i][:, t, :], ident_bf16[:])
+
+        def regroup_latent(i):
+            lat_grouped[i] = work.tile([P, P, PACK], BF16, name="lg", align_bytes=64)
+            nc.vector.tensor_copy(
+                out=lat_grouped[i][:], in_=latt_psum[i][:].rearrange("p t m -> p m t")
+            )
+
+        def quantise_latent(i):
+            lat_codes[i] = kept.tile([P, P], U32, name="lq", align_bytes=64)
+            lat_scales[i] = kept.tile([P, P], U8, name="lsc", align_bytes=64)
+            nc.vector.quantize_mx(
+                out=lat_codes[i][:].bitcast(FP8X4),
+                scales=lat_scales[i][:],
+                in_=lat_grouped[i][:].rearrange("p m t -> p (m t)"),
+            )
+
+        def up_matmul(i):
+            k_psum[i] = psum_k.tile([P, H * D], F32, name="k")
+            v_psum[i] = psum_v.tile([P, H * D], F32, name="v")
+            for half, bank in enumerate((k_psum[i], v_psum[i])):
+                nc.tensor.matmul_mx(
+                    out=bank[:],
+                    lhsT=lat_codes[i][:].bitcast(FP8X4),
+                    lhsT_scale=lat_scales[i][:],
+                    rhs=w_up[:, half * H * D * PACK : (half + 1) * H * D * PACK].bitcast(FP8X4),
+                    rhs_scale=planes[
+                        :, DOWN_PASSES * R + half * H * D : DOWN_PASSES * R + (half + 1) * H * D
+                    ],
+                    start=True,
+                    stop=True,
+                )
+
+        def measure_k(i):
+            squares = work.tile([P, H, D], BF16, name="squares")
+            sums = work.tile([P, H], F32, name="sums")
+            for h in range(H):
+                nc.scalar.activation(
+                    out=squares[:, h, :],
+                    in_=k_psum[i][:, h * D : (h + 1) * D],
+                    func=SQUARE,
+                    accum_out=sums[:, h : h + 1],
+                )
+            rms[i] = kept.tile([P, H], F32, name="rms")
+            nc.scalar.activation(
+                out=rms[i][:], in_=sums[:], func=SQRT, scale=1.0 / D, bias=eps_col[:, 0:1]
+            )
+
+        def copy_v(i):
+            v_out = outs.tile([P, H * D], F32, name="v_out")
+            nc.scalar.copy(out=v_out[:], in_=v_psum[i][:])
+            nc.sync.dma_start(out=v_groups[i // GROUP_TILES, :, i % GROUP_TILES, :], in_=v_out[:])
+
+        def rotate_k(i):
+            rstd = work.tile([P, H], F32, name="rstd")
+            nc.vector.reciprocal(out=rstd[:], in_=rms[i][:])
+            a = i % SEQ_TILES
+            k_pairs = k_psum[i][:].rearrange("m (h j e) -> m h j e", h=H, e=2)
+            same[i] = kept.tile([P, H, PAIRS, 2], F32, name="same")
+            cross[i] = kept.tile([P, H, 2, PAIRS], F32, name="cross")
+            for h in range(H):
+                nc.vector.scalar_tensor_tensor(
+                    out=same[i][:, h].rearrange("m j e -> m (j e)"),
+                    in0=k_psum[i][:, h * D : (h + 1) * D],
+                    scalar=rstd[:, h : h + 1],
+                    in1=table_same[:, a].rearrange("p j e -> p (j e)"),
+                    op0=MULT,
+                    op1=MULT,
+                )
+                for e in range(2):
+                    nc.vector.scalar_tensor_tensor(
+                        out=cross[i][:, h, e, :],
+                        in0=k_pairs[:, h, :, 1 - e],
+                        scalar=rstd[:, h : h + 1],
+                        in1=table_cross[:, a, e, :],
+                        op0=MULT,
+                        op1=MULT,
+                    )
+
+        def add_products(i):
+            k_out = outs.tile([P, H, PAIRS, 2], F32, name="k_out")
+            for h in range(0, H, ADD_HEADS):
+                heads = slice(h, h + ADD_HEADS)
+                nc.gpsimd.tensor_tensor(
+                    out=k_out[:, heads],
+                    in0=same[i][:, heads],
+                    in1=cross[i][:, heads].rearrange("m h e j -> m h j e"),
+                    op=ADD,
+                )
+            nc.sync.dma_start(
+                out=k_groups[i // GROUP_TILES, :, i % GROUP_TILES, :],
+                in_=k_out[:].rearrange("m h j e -> m (h j e)"),
+            )
+
+        def run(stage, i):
+            if 0 <= i < N_TILES:
+                stage(i)
+
+        for r in range(-3, N_TILES + 1):
+            run(transpose_x, r + 3)
+            run(transpose_latent, r + 1)
+            run(down_matmul, r + 2)
+            run(up_matmul, r)
+            run(regroup_x, r + 3)
+            run(round_latent, r + 2)
+            run(measure_k, r)
+            run(copy_v, r)
+            run(rotate_k, r - 1)
+            run(regroup_latent, r + 1)
+            run(quantise_x, r + 3)
+            run(quantise_latent, r + 1)
+            run(add_products, r - 1)

@@ -12,7 +12,7 @@ FP8X4 = mybir.dt.float8_e4m3fn_x4
 MULT = mybir.AluOpType.mult
 ADD = mybir.AluOpType.add
 SQUARE = mybir.ActivationFunctionType.Square
-SQRT = mybir.ActivationFunctionType.Sqrt
+RSQRT = mybir.ActivationFunctionType.Abs_reciprocal_sqrt
 
 P = 128
 PACK = 4
@@ -30,7 +30,6 @@ GROUP_TILES = 4
 N_TILES = TOKENS // P
 N_GROUPS = N_TILES // GROUP_TILES
 SEQ_TILES = SEQ // P
-ADD_HEADS = 2
 
 FLOPS = 2 * TOKENS * (C * R + R * 2 * H * D)
 
@@ -62,12 +61,12 @@ def tile_mla_pa_t_kernel(
         ctx.enter_context(tc.manual_schedule())
         const = ctx.enter_context(tc.tile_pool(name="const", bufs=1))
         work = ctx.enter_context(tc.tile_pool(name="work", bufs=2))
-        kept = ctx.enter_context(tc.tile_pool(name="kept", bufs=3))
+        kept = ctx.enter_context(tc.tile_pool(name="kept", bufs=4))
         outs = ctx.enter_context(tc.tile_pool(name="outs", bufs=6))
-        psum_xt = ctx.enter_context(tc.psum_pool(name="psum_xt", bufs=2))
+        psum_xt = ctx.enter_context(tc.psum_pool(name="psum_xt", bufs=1))
         psum_lat = ctx.enter_context(tc.psum_pool(name="psum_lat", bufs=1))
         psum_latt = ctx.enter_context(tc.psum_pool(name="psum_latt", bufs=1))
-        psum_k = ctx.enter_context(tc.psum_pool(name="psum_k", bufs=2))
+        psum_k = ctx.enter_context(tc.psum_pool(name="psum_k", bufs=3))
         psum_v = ctx.enter_context(tc.psum_pool(name="psum_v", bufs=2))
 
         planes = const.tile([P, DOWN_PASSES * R + 2 * H * D], U8, name="planes", align_bytes=64)
@@ -97,7 +96,7 @@ def tile_mla_pa_t_kernel(
             in_=freqs_sin.rearrange(table_view, p=P, s=GROUP_TILES),
         )
         warm = const.tile([P, 1], F32, name="warm")
-        nc.scalar.activation(out=warm[:], in_=eps_col[:], func=SQRT)
+        nc.scalar.activation(out=warm[:], in_=eps_col[:], func=RSQRT)
 
         x_sb = [const.tile([P, GROUP_TILES, C], BF16, name="x%d" % g) for g in range(N_GROUPS)]
         w_down = const.tile([P, DOWN_PASSES, R * PACK], U8, name="w_down", align_bytes=64)
@@ -157,7 +156,7 @@ def tile_mla_pa_t_kernel(
 
         xt_psum, x_grouped, x_codes, x_scales = {}, {}, {}, {}
         lat_psum, lat_sorted, latt_psum, lat_grouped, lat_codes, lat_scales = {}, {}, {}, {}, {}, {}
-        k_psum, v_psum, rms, same, cross = {}, {}, {}, {}, {}
+        k_psum, v_psum, sums, rstd, same, cross = {}, {}, {}, {}, {}, {}
 
         def transpose_x(i):
             words = x_sb[i // GROUP_TILES][:, i % GROUP_TILES, :].bitcast(F32)
@@ -207,9 +206,15 @@ def tile_mla_pa_t_kernel(
             )
 
         def transpose_latent(i):
-            latt_psum[i] = psum_latt.tile([P, PACK, P], BF16, name="latt")
+            latt_psum[i] = psum_latt.tile([P, PACK, P], F32, name="latt")
             for t in range(PACK):
-                nc.tensor.transpose(latt_psum[i][:, t, :], lat_sorted[i][:, t, :], ident_bf16[:])
+                nc.tensor.matmul(
+                    out=latt_psum[i][:, t, :],
+                    lhsT=lat_sorted[i][:, t, :],
+                    rhs=ident_bf16[:],
+                    start=True,
+                    stop=True,
+                )
 
         def regroup_latent(i):
             lat_grouped[i] = work.tile([P, P, PACK], BF16, name="lg", align_bytes=64)
@@ -242,19 +247,21 @@ def tile_mla_pa_t_kernel(
                     stop=True,
                 )
 
-        def measure_k(i):
+        def sum_squares(i):
             squares = work.tile([P, H, D], BF16, name="squares")
-            sums = work.tile([P, H], F32, name="sums")
+            sums[i] = work.tile([P, H], F32, name="sums")
             for h in range(H):
                 nc.scalar.activation(
                     out=squares[:, h, :],
                     in_=k_psum[i][:, h * D : (h + 1) * D],
                     func=SQUARE,
-                    accum_out=sums[:, h : h + 1],
+                    accum_out=sums[i][:, h : h + 1],
                 )
-            rms[i] = kept.tile([P, H], F32, name="rms")
+
+        def inverse_rms(i):
+            rstd[i] = kept.tile([P, H], F32, name="rstd")
             nc.scalar.activation(
-                out=rms[i][:], in_=sums[:], func=SQRT, scale=1.0 / D, bias=eps_col[:, 0:1]
+                out=rstd[i][:], in_=sums[i][:], func=RSQRT, scale=1.0 / D, bias=eps_col[:, 0:1]
             )
 
         def copy_v(i):
@@ -262,42 +269,40 @@ def tile_mla_pa_t_kernel(
             nc.scalar.copy(out=v_out[:], in_=v_psum[i][:])
             nc.sync.dma_start(out=v_groups[i // GROUP_TILES, :, i % GROUP_TILES, :], in_=v_out[:])
 
-        def rotate_k(i):
-            rstd = work.tile([P, H], F32, name="rstd")
-            nc.vector.reciprocal(out=rstd[:], in_=rms[i][:])
-            a = i % SEQ_TILES
-            k_pairs = k_psum[i][:].rearrange("m (h j e) -> m h j e", h=H, e=2)
+        def rotate_same(i):
             same[i] = kept.tile([P, H, PAIRS, 2], F32, name="same")
-            cross[i] = kept.tile([P, H, 2, PAIRS], F32, name="cross")
             for h in range(H):
                 nc.vector.scalar_tensor_tensor(
                     out=same[i][:, h].rearrange("m j e -> m (j e)"),
                     in0=k_psum[i][:, h * D : (h + 1) * D],
-                    scalar=rstd[:, h : h + 1],
-                    in1=table_same[:, a].rearrange("p j e -> p (j e)"),
+                    scalar=rstd[i][:, h : h + 1],
+                    in1=table_same[:, i % SEQ_TILES].rearrange("p j e -> p (j e)"),
                     op0=MULT,
                     op1=MULT,
                 )
+
+        def rotate_cross(i):
+            k_pairs = k_psum[i][:].rearrange("m (h j e) -> m h j e", h=H, e=2)
+            cross[i] = kept.tile([P, H, 2, PAIRS], F32, name="cross")
+            for h in range(H):
                 for e in range(2):
                     nc.vector.scalar_tensor_tensor(
                         out=cross[i][:, h, e, :],
                         in0=k_pairs[:, h, :, 1 - e],
-                        scalar=rstd[:, h : h + 1],
-                        in1=table_cross[:, a, e, :],
+                        scalar=rstd[i][:, h : h + 1],
+                        in1=table_cross[:, i % SEQ_TILES, e, :],
                         op0=MULT,
                         op1=MULT,
                     )
 
         def add_products(i):
             k_out = outs.tile([P, H, PAIRS, 2], F32, name="k_out")
-            for h in range(0, H, ADD_HEADS):
-                heads = slice(h, h + ADD_HEADS)
-                nc.gpsimd.tensor_tensor(
-                    out=k_out[:, heads],
-                    in0=same[i][:, heads],
-                    in1=cross[i][:, heads].rearrange("m h e j -> m h j e"),
-                    op=ADD,
-                )
+            nc.gpsimd.tensor_tensor(
+                out=k_out[:],
+                in0=same[i][:],
+                in1=cross[i][:].rearrange("m h e j -> m h j e"),
+                op=ADD,
+            )
             nc.sync.dma_start(
                 out=k_groups[i // GROUP_TILES, :, i % GROUP_TILES, :],
                 in_=k_out[:].rearrange("m h j e -> m (h j e)"),
@@ -307,17 +312,19 @@ def tile_mla_pa_t_kernel(
             if 0 <= i < N_TILES:
                 stage(i)
 
-        for r in range(-3, N_TILES + 1):
-            run(transpose_x, r + 3)
-            run(transpose_latent, r + 1)
-            run(down_matmul, r + 2)
+        for r in range(-6, N_TILES + 2):
             run(up_matmul, r)
-            run(regroup_x, r + 3)
-            run(round_latent, r + 2)
-            run(measure_k, r)
+            run(transpose_x, r + 6)
+            run(down_matmul, r + 4)
+            run(transpose_latent, r + 3)
+            run(sum_squares, r)
             run(copy_v, r)
-            run(rotate_k, r - 1)
-            run(regroup_latent, r + 1)
-            run(quantise_x, r + 3)
-            run(quantise_latent, r + 1)
-            run(add_products, r - 1)
+            run(inverse_rms, r)
+            run(regroup_x, r + 6)
+            run(round_latent, r + 4)
+            run(rotate_same, r - 2)
+            run(rotate_cross, r - 1)
+            run(regroup_latent, r + 2)
+            run(quantise_x, r + 5)
+            run(quantise_latent, r + 2)
+            run(add_products, r - 2)

@@ -132,31 +132,31 @@ def tile_mla_pa_t_kernel(
         for g in range(1, N_GROUPS):
             nc.sync.dma_start(out=x_sb[g][:], in_=x_groups[g])
 
-        gain_cross = const.tile([P, 2, PAIRS], F32, name="gain_cross")
+        gain_signed = const.tile([P, PAIRS, 2], F32, name="gain_signed")
+        nc.gpsimd.tensor_copy(out=gain_signed[:, :, 0], in_=gain[:, :, 0])
         nc.gpsimd.tensor_scalar(
-            out=gain_cross[:, 0, :], in0=gain[:, :, 1], scalar1=-1.0, scalar2=0.0, op0=MULT, op1=ADD
+            out=gain_signed[:, :, 1], in0=gain[:, :, 1], scalar1=-1.0, scalar2=0.0, op0=MULT, op1=ADD
         )
-        nc.gpsimd.tensor_copy(out=gain_cross[:, 1, :], in_=gain[:, :, 0])
-        table_same = const.tile([P, SEQ_TILES, PAIRS, 2], F32, name="table_same")
-        table_cross = const.tile([P, SEQ_TILES, 2, PAIRS], F32, name="table_cross")
+        table = const.tile([P, SEQ_TILES, 2, PAIRS, 2], F32, name="table")
         for a in range(0, SEQ_TILES, GROUP_TILES):
             tiles = slice(a, a + GROUP_TILES)
+            shape = [P, GROUP_TILES, PAIRS, 2]
             nc.gpsimd.tensor_tensor(
-                out=table_same[:, tiles],
-                in0=cos_sb[:, tiles, :].unsqueeze(3).to_broadcast([P, GROUP_TILES, PAIRS, 2]),
-                in1=gain[:].unsqueeze(1).to_broadcast([P, GROUP_TILES, PAIRS, 2]),
+                out=table[:, tiles, 0],
+                in0=cos_sb[:, tiles, :].unsqueeze(3).to_broadcast(shape),
+                in1=gain[:].unsqueeze(1).to_broadcast(shape),
                 op=MULT,
             )
             nc.gpsimd.tensor_tensor(
-                out=table_cross[:, tiles],
-                in0=sin_sb[:, tiles, :].unsqueeze(2).to_broadcast([P, GROUP_TILES, 2, PAIRS]),
-                in1=gain_cross[:].unsqueeze(1).to_broadcast([P, GROUP_TILES, 2, PAIRS]),
+                out=table[:, tiles, 1],
+                in0=sin_sb[:, tiles, :].unsqueeze(3).to_broadcast(shape),
+                in1=gain_signed[:].unsqueeze(1).to_broadcast(shape),
                 op=MULT,
             )
 
         xt_psum, x_grouped, x_codes, x_scales = {}, {}, {}, {}
         lat_psum, lat_sorted, latt_psum, lat_grouped, lat_codes, lat_scales = {}, {}, {}, {}, {}, {}
-        k_psum, v_psum, sums, rstd, same, cross = {}, {}, {}, {}, {}, {}
+        k_psum, v_psum, sums, rstd, products = {}, {}, {}, {}, {}
 
         def transpose_x(i):
             words = x_sb[i // GROUP_TILES][:, i % GROUP_TILES, :].bitcast(F32)
@@ -269,39 +269,29 @@ def tile_mla_pa_t_kernel(
             nc.scalar.copy(out=v_out[:], in_=v_psum[i][:])
             nc.sync.dma_start(out=v_groups[i // GROUP_TILES, :, i % GROUP_TILES, :], in_=v_out[:])
 
-        def rotate_same(i):
-            same[i] = kept.tile([P, H, PAIRS, 2], F32, name="same")
-            for h in range(H):
+        def rotate_heads(i, heads):
+            for h in heads:
                 nc.vector.scalar_tensor_tensor(
-                    out=same[i][:, h].rearrange("m j e -> m (j e)"),
-                    in0=k_psum[i][:, h * D : (h + 1) * D],
+                    out=products[i][:, h],
+                    in0=k_psum[i][:, h * D : (h + 1) * D].unsqueeze(1).to_broadcast([P, 2, D]),
                     scalar=rstd[i][:, h : h + 1],
-                    in1=table_same[:, i % SEQ_TILES].rearrange("p j e -> p (j e)"),
+                    in1=table[:, i % SEQ_TILES].rearrange("p w j e -> p w (j e)"),
                     op0=MULT,
                     op1=MULT,
                 )
 
-        def rotate_cross(i):
-            k_pairs = k_psum[i][:].rearrange("m (h j e) -> m h j e", h=H, e=2)
-            cross[i] = kept.tile([P, H, 2, PAIRS], F32, name="cross")
-            for h in range(H):
-                for e in range(2):
-                    nc.vector.scalar_tensor_tensor(
-                        out=cross[i][:, h, e, :],
-                        in0=k_pairs[:, h, :, 1 - e],
-                        scalar=rstd[i][:, h : h + 1],
-                        in1=table_cross[:, i % SEQ_TILES, e, :],
-                        op0=MULT,
-                        op1=MULT,
-                    )
+        def rotate_first_heads(i):
+            products[i] = kept.tile([P, H, 2, D], F32, name="products")
+            rotate_heads(i, range(0, H // 2))
+
+        def rotate_last_heads(i):
+            rotate_heads(i, range(H // 2, H))
 
         def add_products(i):
+            pairs = products[i][:].rearrange("m h w (j e) -> m h w j e", e=2)
             k_out = outs.tile([P, H, PAIRS, 2], F32, name="k_out")
             nc.gpsimd.tensor_tensor(
-                out=k_out[:],
-                in0=same[i][:],
-                in1=cross[i][:].rearrange("m h e j -> m h j e"),
-                op=ADD,
+                out=k_out[:], in0=pairs[:, :, 0, :, :], in1=pairs[:, :, 1, :, ::-1], op=ADD
             )
             nc.sync.dma_start(
                 out=k_groups[i // GROUP_TILES, :, i % GROUP_TILES, :],
@@ -322,8 +312,8 @@ def tile_mla_pa_t_kernel(
             run(inverse_rms, r)
             run(regroup_x, r + 6)
             run(round_latent, r + 4)
-            run(rotate_same, r - 2)
-            run(rotate_cross, r - 1)
+            run(rotate_last_heads, r - 2)
+            run(rotate_first_heads, r - 1)
             run(regroup_latent, r + 2)
             run(quantise_x, r + 5)
             run(quantise_latent, r + 2)

@@ -62,11 +62,11 @@ def tile_mla_pa_t_kernel(
         const = ctx.enter_context(tc.tile_pool(name="const", bufs=1))
         work = ctx.enter_context(tc.tile_pool(name="work", bufs=2))
         kept = ctx.enter_context(tc.tile_pool(name="kept", bufs=4))
-        outs = ctx.enter_context(tc.tile_pool(name="outs", bufs=6))
-        psum_xt = ctx.enter_context(tc.psum_pool(name="psum_xt", bufs=1))
+        outs = ctx.enter_context(tc.tile_pool(name="outs", bufs=8))
+        psum_xt = ctx.enter_context(tc.psum_pool(name="psum_xt", bufs=2))
         psum_lat = ctx.enter_context(tc.psum_pool(name="psum_lat", bufs=1))
         psum_latt = ctx.enter_context(tc.psum_pool(name="psum_latt", bufs=1))
-        psum_k = ctx.enter_context(tc.psum_pool(name="psum_k", bufs=3))
+        psum_k = ctx.enter_context(tc.psum_pool(name="psum_k", bufs=2))
         psum_v = ctx.enter_context(tc.psum_pool(name="psum_v", bufs=2))
 
         planes = const.tile([P, DOWN_PASSES * R + 2 * H * D], U8, name="planes", align_bytes=64)
@@ -80,28 +80,20 @@ def tile_mla_pa_t_kernel(
         ident_bf16 = const.tile([P, P], BF16, name="ident_bf16")
         masks.make_identity(nc, ident_bf16[:])
 
-        cos_sb = const.tile([P, SEQ_TILES, PAIRS], BF16, name="cos_sb")
-        sin_sb = const.tile([P, SEQ_TILES, PAIRS], BF16, name="sin_sb")
-        gain = const.tile([P, PAIRS, 2], BF16, name="gain")
-        nc.scalar.dma_start(
-            out=gain[:].rearrange("p j e -> p (j e)"), in_=k_norm_w.partition_broadcast(P)
-        )
-        table_view = "(a p s) j -> p a s j"
-        nc.scalar.dma_start(
-            out=cos_sb[:].rearrange("p (a s) j -> p a s j", s=GROUP_TILES),
-            in_=freqs_cos.rearrange(table_view, p=P, s=GROUP_TILES),
-        )
-        nc.scalar.dma_start(
-            out=sin_sb[:].rearrange("p (a s) j -> p a s j", s=GROUP_TILES),
-            in_=freqs_sin.rearrange(table_view, p=P, s=GROUP_TILES),
-        )
         warm = const.tile([P, 1], F32, name="warm")
         nc.scalar.activation(out=warm[:], in_=eps_col[:], func=RSQRT)
 
+        gain_row = const.tile([P, D], BF16, name="gain_row")
+        nc.vector.memset(gain_row[:], 0.0)
+        ones = const.tile([P, P], BF16, name="ones")
+        nc.vector.memset(ones[:], 1.0)
+        cos_sb = const.tile([P, SEQ_TILES, PAIRS], BF16, name="cos_sb")
+        sin_sb = const.tile([P, SEQ_TILES, PAIRS], BF16, name="sin_sb")
         x_sb = [const.tile([P, GROUP_TILES, C], BF16, name="x%d" % g) for g in range(N_GROUPS)]
         w_down = const.tile([P, DOWN_PASSES, R * PACK], U8, name="w_down", align_bytes=64)
         w_up = const.tile([P, 2 * H * D * PACK], U8, name="w_up", align_bytes=64)
 
+        nc.sync.dma_start(out=gain_row[0:1, :], in_=k_norm_w.unsqueeze(0))
         nc.sync.dma_start(out=x_sb[0][:, 0, :], in_=x_groups[0, :, 0, :])
         down_scales_i32 = w_kv_down_scales.bitcast(I32)
         for quad in range(4):
@@ -119,6 +111,16 @@ def tile_mla_pa_t_kernel(
         )
         for s in range(1, GROUP_TILES):
             nc.sync.dma_start(out=x_sb[0][:, s, :], in_=x_groups[0, :, s, :])
+        nc.sync.dma_start(out=x_sb[1][:], in_=x_groups[1])
+        table_view = "(a p s) j -> p a s j"
+        nc.sync.dma_start(
+            out=cos_sb[:].rearrange("p (a s) j -> p a s j", s=GROUP_TILES),
+            in_=freqs_cos.rearrange(table_view, p=P, s=GROUP_TILES),
+        )
+        nc.sync.dma_start(
+            out=sin_sb[:].rearrange("p (a s) j -> p a s j", s=GROUP_TILES),
+            in_=freqs_sin.rearrange(table_view, p=P, s=GROUP_TILES),
+        )
         up_scales_i32 = w_kv_up_scales.bitcast(I32)
         for quad in range(4):
             nc.sync.dma_start(
@@ -129,8 +131,13 @@ def tile_mla_pa_t_kernel(
             out=w_up[:].bitcast(I32),
             in_=w_kv_up_words[0].rearrange("p n t -> p (n t)").bitcast(I32),
         )
-        for g in range(1, N_GROUPS):
+        for g in range(2, N_GROUPS):
             nc.sync.dma_start(out=x_sb[g][:], in_=x_groups[g])
+
+        gain_psum = psum_latt.tile([P, PACK, P], F32, name="latt")
+        nc.tensor.matmul(out=gain_psum[:, 0, :], lhsT=ones[:], rhs=gain_row[:], start=True, stop=True)
+        gain = const.tile([P, PAIRS, 2], F32, name="gain")
+        nc.vector.tensor_copy(out=gain[:].rearrange("p j e -> p (j e)"), in_=gain_psum[:, 0, :])
 
         gain_signed = const.tile([P, PAIRS, 2], F32, name="gain_signed")
         nc.gpsimd.tensor_copy(out=gain_signed[:, :, 0], in_=gain[:, :, 0])
@@ -269,8 +276,9 @@ def tile_mla_pa_t_kernel(
             nc.scalar.copy(out=v_out[:], in_=v_psum[i][:])
             nc.sync.dma_start(out=v_groups[i // GROUP_TILES, :, i % GROUP_TILES, :], in_=v_out[:])
 
-        def rotate_heads(i, heads):
-            for h in heads:
+        def rotate_k(i):
+            products[i] = kept.tile([P, H, 2, D], F32, name="products")
+            for h in range(H):
                 nc.vector.scalar_tensor_tensor(
                     out=products[i][:, h],
                     in0=k_psum[i][:, h * D : (h + 1) * D].unsqueeze(1).to_broadcast([P, 2, D]),
@@ -279,13 +287,6 @@ def tile_mla_pa_t_kernel(
                     op0=MULT,
                     op1=MULT,
                 )
-
-        def rotate_first_heads(i):
-            products[i] = kept.tile([P, H, 2, D], F32, name="products")
-            rotate_heads(i, range(0, H // 2))
-
-        def rotate_last_heads(i):
-            rotate_heads(i, range(H // 2, H))
 
         def add_products(i):
             pairs = products[i][:].rearrange("m h w (j e) -> m h w j e", e=2)
@@ -302,7 +303,7 @@ def tile_mla_pa_t_kernel(
             if 0 <= i < N_TILES:
                 stage(i)
 
-        for r in range(-6, N_TILES + 2):
+        for r in range(-6, N_TILES + 1):
             run(up_matmul, r)
             run(transpose_x, r + 6)
             run(down_matmul, r + 4)
@@ -312,9 +313,8 @@ def tile_mla_pa_t_kernel(
             run(inverse_rms, r)
             run(regroup_x, r + 6)
             run(round_latent, r + 4)
-            run(rotate_last_heads, r - 2)
-            run(rotate_first_heads, r - 1)
             run(regroup_latent, r + 2)
+            run(rotate_k, r - 1)
             run(quantise_x, r + 5)
             run(quantise_latent, r + 2)
-            run(add_products, r - 2)
+            run(add_products, r - 1)

@@ -64,8 +64,7 @@ def tile_mla_pa_t_kernel(
         kept = ctx.enter_context(tc.tile_pool(name="kept", bufs=4))
         outs = ctx.enter_context(tc.tile_pool(name="outs", bufs=8))
         psum_xt = ctx.enter_context(tc.psum_pool(name="psum_xt", bufs=2))
-        psum_lat = ctx.enter_context(tc.psum_pool(name="psum_lat", bufs=1))
-        psum_latt = ctx.enter_context(tc.psum_pool(name="psum_latt", bufs=1))
+        psum_latt = ctx.enter_context(tc.psum_pool(name="psum_latt", bufs=2))
         psum_k = ctx.enter_context(tc.psum_pool(name="psum_k", bufs=2))
         psum_v = ctx.enter_context(tc.psum_pool(name="psum_v", bufs=2))
 
@@ -77,8 +76,6 @@ def tile_mla_pa_t_kernel(
 
         ident_f32 = const.tile([P, P], F32, name="ident_f32")
         masks.make_identity(nc, ident_f32[:])
-        ident_bf16 = const.tile([P, P], BF16, name="ident_bf16")
-        masks.make_identity(nc, ident_bf16[:])
 
         warm = const.tile([P, 1], F32, name="warm")
         nc.scalar.activation(out=warm[:], in_=eps_col[:], func=RSQRT)
@@ -134,6 +131,17 @@ def tile_mla_pa_t_kernel(
         for g in range(2, N_GROUPS):
             nc.sync.dma_start(out=x_sb[g][:], in_=x_groups[g])
 
+        w_down_sorted = const.tile([P, DOWN_PASSES, PACK, P], I32, name="w_down_sorted", align_bytes=64)
+        planes_sorted = const.tile([P, DOWN_PASSES, PACK, P], U8, name="planes_sorted", align_bytes=64)
+        nc.gpsimd.tensor_copy(
+            out=planes_sorted[:],
+            in_=planes[:, 0 : DOWN_PASSES * R].rearrange("p (g m t) -> p g t m", g=DOWN_PASSES, t=PACK),
+        )
+        nc.vector.tensor_copy(
+            out=w_down_sorted[:],
+            in_=w_down[:].bitcast(I32).rearrange("p g (m t) -> p g t m", t=PACK),
+        )
+
         gain_psum = psum_latt.tile([P, PACK, P], F32, name="latt")
         nc.tensor.matmul(out=gain_psum[:, 0, :], lhsT=ones[:], rhs=gain_row[:], start=True, stop=True)
         gain = const.tile([P, PAIRS, 2], F32, name="gain")
@@ -162,7 +170,7 @@ def tile_mla_pa_t_kernel(
             )
 
         xt_psum, x_grouped, x_codes, x_scales = {}, {}, {}, {}
-        lat_psum, lat_sorted, latt_psum, lat_grouped, lat_codes, lat_scales = {}, {}, {}, {}, {}, {}
+        latt_psum, lat_grouped, lat_codes, lat_scales = {}, {}, {}, {}
         k_psum, v_psum, sums, rstd, products = {}, {}, {}, {}, {}
 
         def transpose_x(i):
@@ -193,35 +201,19 @@ def tile_mla_pa_t_kernel(
             )
 
         def down_matmul(i):
-            lat_psum[i] = psum_lat.tile([P, R], F32, name="lat")
-            for g in range(DOWN_PASSES):
-                tokens = slice(g * P, (g + 1) * P)
-                nc.tensor.matmul_mx(
-                    out=lat_psum[i][:],
-                    lhsT=x_codes[i][:, tokens].bitcast(FP8X4),
-                    lhsT_scale=x_scales[i][:, tokens],
-                    rhs=w_down[:, g, :].bitcast(FP8X4),
-                    rhs_scale=planes[:, g * R : (g + 1) * R],
-                    start=(g == 0),
-                    stop=(g == DOWN_PASSES - 1),
-                )
-
-        def round_latent(i):
-            lat_sorted[i] = work.tile([P, PACK, P], BF16, name="ls")
-            nc.scalar.copy(
-                out=lat_sorted[i][:], in_=lat_psum[i][:].rearrange("m (p t) -> m t p", t=PACK)
-            )
-
-        def transpose_latent(i):
             latt_psum[i] = psum_latt.tile([P, PACK, P], F32, name="latt")
             for t in range(PACK):
-                nc.tensor.matmul(
-                    out=latt_psum[i][:, t, :],
-                    lhsT=lat_sorted[i][:, t, :],
-                    rhs=ident_bf16[:],
-                    start=True,
-                    stop=True,
-                )
+                for g in range(DOWN_PASSES):
+                    tokens = slice(g * P, (g + 1) * P)
+                    nc.tensor.matmul_mx(
+                        out=latt_psum[i][:, t, :],
+                        lhsT=w_down_sorted[:, g, t, :].bitcast(FP8X4),
+                        lhsT_scale=planes_sorted[:, g, t, :],
+                        rhs=x_codes[i][:, tokens].bitcast(FP8X4),
+                        rhs_scale=x_scales[i][:, tokens],
+                        start=(g == 0),
+                        stop=(g == DOWN_PASSES - 1),
+                    )
 
         def regroup_latent(i):
             lat_grouped[i] = work.tile([P, P, PACK], BF16, name="lg", align_bytes=64)
@@ -303,18 +295,16 @@ def tile_mla_pa_t_kernel(
             if 0 <= i < N_TILES:
                 stage(i)
 
-        for r in range(-6, N_TILES + 1):
+        for r in range(-5, N_TILES + 1):
             run(up_matmul, r)
-            run(transpose_x, r + 6)
-            run(down_matmul, r + 4)
-            run(transpose_latent, r + 3)
+            run(transpose_x, r + 5)
+            run(down_matmul, r + 3)
             run(sum_squares, r)
             run(copy_v, r)
             run(inverse_rms, r)
-            run(regroup_x, r + 6)
-            run(round_latent, r + 4)
+            run(regroup_x, r + 5)
             run(regroup_latent, r + 2)
             run(rotate_k, r - 1)
-            run(quantise_x, r + 5)
+            run(quantise_x, r + 4)
             run(quantise_latent, r + 2)
             run(add_products, r - 1)

@@ -133,7 +133,7 @@ def tile_mla_pa_t_kernel(
 
         w_down_sorted = const.tile([P, DOWN_PASSES, PACK, P], I32, name="w_down_sorted", align_bytes=64)
         planes_sorted = const.tile([P, DOWN_PASSES, PACK, P], U8, name="planes_sorted", align_bytes=64)
-        nc.gpsimd.tensor_copy(
+        nc.vector.tensor_copy(
             out=planes_sorted[:],
             in_=planes[:, 0 : DOWN_PASSES * R].rearrange("p (g m t) -> p g t m", g=DOWN_PASSES, t=PACK),
         )
@@ -215,11 +215,17 @@ def tile_mla_pa_t_kernel(
                         stop=(g == DOWN_PASSES - 1),
                     )
 
+        def on_scalar(i):
+            return i % 4 == 3
+
         def regroup_latent(i):
             lat_grouped[i] = work.tile([P, P, PACK], BF16, name="lg", align_bytes=64)
-            nc.vector.tensor_copy(
-                out=lat_grouped[i][:], in_=latt_psum[i][:].rearrange("p t m -> p m t")
-            )
+            if on_scalar(i):
+                nc.scalar.copy(out=lat_grouped[i][:], in_=latt_psum[i][:].rearrange("p t m -> p m t"))
+            else:
+                nc.vector.tensor_copy(
+                    out=lat_grouped[i][:], in_=latt_psum[i][:].rearrange("p t m -> p m t")
+                )
 
         def quantise_latent(i):
             lat_codes[i] = kept.tile([P, P], U32, name="lq", align_bytes=64)
@@ -299,11 +305,14 @@ def tile_mla_pa_t_kernel(
             run(up_matmul, r)
             run(transpose_x, r + 5)
             run(down_matmul, r + 3)
+            if on_scalar(r + 2):
+                run(regroup_latent, r + 2)
             run(sum_squares, r)
             run(copy_v, r)
             run(inverse_rms, r)
             run(regroup_x, r + 5)
-            run(regroup_latent, r + 2)
+            if not on_scalar(r + 2):
+                run(regroup_latent, r + 2)
             run(rotate_k, r - 1)
             run(quantise_x, r + 4)
             run(quantise_latent, r + 2)

@@ -301,19 +301,16 @@ def tile_mla_pa_t_kernel(
             if 0 <= i < N_TILES:
                 stage(i)
 
-        for r in range(-5, N_TILES + 1):
+        for r in range(-6, N_TILES + 1):
+            run(regroup_latent, r + 2)
             run(up_matmul, r)
-            run(transpose_x, r + 5)
-            run(down_matmul, r + 3)
-            if on_scalar(r + 2):
-                run(regroup_latent, r + 2)
+            run(transpose_x, r + 6)
+            run(down_matmul, r + 4)
             run(sum_squares, r)
             run(copy_v, r)
             run(inverse_rms, r)
-            run(regroup_x, r + 5)
-            if not on_scalar(r + 2):
-                run(regroup_latent, r + 2)
+            run(regroup_x, r + 6)
             run(rotate_k, r - 1)
-            run(quantise_x, r + 4)
+            run(quantise_x, r + 5)
             run(quantise_latent, r + 2)
             run(add_products, r - 1)

@@ -30,6 +30,8 @@ GROUP_TILES = 4
 N_TILES = TOKENS // P
 N_GROUPS = N_TILES // GROUP_TILES
 SEQ_TILES = SEQ // P
+X_LEAD = 6
+FIRST_SPARE = N_TILES - X_LEAD
 
 FLOPS = 2 * TOKENS * (C * R + R * 2 * H * D)
 
@@ -237,7 +239,10 @@ def tile_mla_pa_t_kernel(
             )
 
         def up_matmul(i):
-            k_psum[i] = psum_k.tile([P, H * D], F32, name="k")
+            if i >= FIRST_SPARE and (i - FIRST_SPARE) % 4 < 2:
+                k_psum[i] = psum_xt.tile([P, H * D], F32, name="xt")
+            else:
+                k_psum[i] = psum_k.tile([P, H * D], F32, name="k")
             v_psum[i] = psum_v.tile([P, H * D], F32, name="v")
             for half, bank in enumerate((k_psum[i], v_psum[i])):
                 nc.tensor.matmul_mx(
@@ -289,7 +294,8 @@ def tile_mla_pa_t_kernel(
         def add_products(i):
             pairs = products[i][:].rearrange("m h w (j e) -> m h w j e", e=2)
             k_out = outs.tile([P, H, PAIRS, 2], F32, name="k_out")
-            nc.gpsimd.tensor_tensor(
+            adder = nc.vector if i == N_TILES - 1 else nc.gpsimd
+            adder.tensor_tensor(
                 out=k_out[:], in0=pairs[:, :, 0, :, :], in1=pairs[:, :, 1, :, ::-1], op=ADD
             )
             nc.sync.dma_start(
@@ -301,15 +307,19 @@ def tile_mla_pa_t_kernel(
             if 0 <= i < N_TILES:
                 stage(i)
 
-        for r in range(-6, N_TILES + 1):
+        for r in range(-X_LEAD, N_TILES + 1):
             run(regroup_latent, r + 2)
             run(up_matmul, r)
-            run(transpose_x, r + 6)
+            run(transpose_x, r + X_LEAD)
             run(down_matmul, r + 4)
             run(sum_squares, r)
-            run(copy_v, r)
-            run(inverse_rms, r)
-            run(regroup_x, r + 6)
+            if r < FIRST_SPARE:
+                run(copy_v, r)
+                run(inverse_rms, r)
+                run(regroup_x, r + X_LEAD)
+            else:
+                run(inverse_rms, r)
+                run(copy_v, r)
             run(rotate_k, r - 1)
             run(quantise_x, r + 5)
             run(quantise_latent, r + 2)

@@ -218,7 +218,7 @@ def tile_mla_pa_t_kernel(
                     )
 
         def on_scalar(i):
-            return i % 4 == 3
+            return i % 3 == 2
 
         def regroup_latent(i):
             lat_grouped[i] = work.tile([P, P, PACK], BF16, name="lg", align_bytes=64)

@@ -31,6 +31,7 @@ N_TILES = TOKENS // P
 N_GROUPS = N_TILES // GROUP_TILES
 SEQ_TILES = SEQ // P
 X_LEAD = 6
+WARM_BEHIND_TILE = (3, 1)
 FIRST_SPARE = N_TILES - X_LEAD
 
 FLOPS = 2 * TOKENS * (C * R + R * 2 * H * D)
@@ -86,6 +87,15 @@ def tile_mla_pa_t_kernel(
         nc.vector.memset(gain_row[:], 0.0)
         ones = const.tile([P, P], BF16, name="ones")
         nc.vector.memset(ones[:], 1.0)
+        zeros = const.tile([P, H * D], BF16, name="zeros")
+        nc.vector.memset(zeros[:], 0.0)
+
+        def keep_warm(count):
+            bank = psum_v.tile([P, H * D], F32, name="v")
+            for n in range(count):
+                nc.tensor.matmul(out=bank[:], lhsT=ones[:], rhs=zeros[:], start=True, stop=True)
+
+        keep_warm(4)
         cos_sb = const.tile([P, SEQ_TILES, PAIRS], BF16, name="cos_sb")
         sin_sb = const.tile([P, SEQ_TILES, PAIRS], BF16, name="sin_sb")
         x_sb = [const.tile([P, GROUP_TILES, C], BF16, name="x%d" % g) for g in range(N_GROUPS)]
@@ -311,6 +321,8 @@ def tile_mla_pa_t_kernel(
             run(regroup_latent, r + 2)
             run(up_matmul, r)
             run(transpose_x, r + X_LEAD)
+            if r + X_LEAD < len(WARM_BEHIND_TILE):
+                keep_warm(WARM_BEHIND_TILE[r + X_LEAD])
             run(down_matmul, r + 4)
             run(sum_squares, r)
             if r < FIRST_SPARE:

@@ -102,8 +102,8 @@ def tile_mla_pa_t_kernel(
         w_down = const.tile([P, DOWN_PASSES, R * PACK], U8, name="w_down", align_bytes=64)
         w_up = const.tile([P, 2 * H * D * PACK], U8, name="w_up", align_bytes=64)
 
-        nc.sync.dma_start(out=gain_row[0:1, :], in_=k_norm_w.unsqueeze(0))
         nc.sync.dma_start(out=x_sb[0][:, 0, :], in_=x_groups[0, :, 0, :])
+        nc.sync.dma_start(out=gain_row[0:1, :], in_=k_norm_w.unsqueeze(0))
         down_scales_i32 = w_kv_down_scales.bitcast(I32)
         for quad in range(4):
             nc.sync.dma_start(
@@ -289,6 +289,14 @@ def tile_mla_pa_t_kernel(
             nc.scalar.copy(out=v_out[:], in_=v_psum[i][:])
             nc.sync.dma_start(out=v_groups[i // GROUP_TILES, :, i % GROUP_TILES, :], in_=v_out[:])
 
+        def copy_v_round_rstd(i):
+            half = H * D // 2
+            v_out = outs.tile([P, H * D], F32, name="v_out")
+            nc.scalar.copy(out=v_out[:, 0:half], in_=v_psum[i][:, 0:half])
+            inverse_rms(i)
+            nc.scalar.copy(out=v_out[:, half:], in_=v_psum[i][:, half:])
+            nc.sync.dma_start(out=v_groups[i // GROUP_TILES, :, i % GROUP_TILES, :], in_=v_out[:])
+
         def rotate_k(i):
             products[i] = kept.tile([P, H, 2, D], F32, name="products")
             for h in range(H):
@@ -304,14 +312,27 @@ def tile_mla_pa_t_kernel(
         def add_products(i):
             pairs = products[i][:].rearrange("m h w (j e) -> m h w j e", e=2)
             k_out = outs.tile([P, H, PAIRS, 2], F32, name="k_out")
-            adder = nc.vector if i == N_TILES - 1 else nc.gpsimd
-            adder.tensor_tensor(
-                out=k_out[:], in0=pairs[:, :, 0, :, :], in1=pairs[:, :, 1, :, ::-1], op=ADD
-            )
-            nc.sync.dma_start(
-                out=k_groups[i // GROUP_TILES, :, i % GROUP_TILES, :],
-                in_=k_out[:].rearrange("m h j e -> m (h j e)"),
-            )
+            if i < N_TILES - 1:
+                nc.gpsimd.tensor_tensor(
+                    out=k_out[:], in0=pairs[:, :, 0, :, :], in1=pairs[:, :, 1, :, ::-1], op=ADD
+                )
+                nc.sync.dma_start(
+                    out=k_groups[i // GROUP_TILES, :, i % GROUP_TILES, :],
+                    in_=k_out[:].rearrange("m h j e -> m (h j e)"),
+                )
+                return
+            for first in range(0, H, 2):
+                heads = slice(first, first + 2)
+                nc.vector.tensor_tensor(
+                    out=k_out[:, heads],
+                    in0=pairs[:, heads, 0, :, :],
+                    in1=pairs[:, heads, 1, :, ::-1],
+                    op=ADD,
+                )
+                nc.sync.dma_start(
+                    out=k_groups[i // GROUP_TILES, :, i % GROUP_TILES, first * D : (first + 2) * D],
+                    in_=k_out[:, heads].rearrange("m h j e -> m (h j e)"),
+                )
 
         def run(stage, i):
             if 0 <= i < N_TILES:
@@ -330,8 +351,7 @@ def tile_mla_pa_t_kernel(
                 run(inverse_rms, r)
                 run(regroup_x, r + X_LEAD)
             else:
-                run(inverse_rms, r)
-                run(copy_v, r)
+                run(copy_v_round_rstd, r)
             run(rotate_k, r - 1)
             run(quantise_x, r + 5)
             run(quantise_latent, r + 2)

@@ -32,6 +32,7 @@ N_GROUPS = N_TILES // GROUP_TILES
 SEQ_TILES = SEQ // P
 X_LEAD = 6
 WARM_BEHIND_TILE = (3, 1)
+HEAD = 4
 FIRST_SPARE = N_TILES - X_LEAD
 
 FLOPS = 2 * TOKENS * (C * R + R * 2 * H * D)
@@ -103,7 +104,6 @@ def tile_mla_pa_t_kernel(
         w_up = const.tile([P, 2 * H * D * PACK], U8, name="w_up", align_bytes=64)
 
         nc.sync.dma_start(out=x_sb[0][:, 0, :], in_=x_groups[0, :, 0, :])
-        nc.sync.dma_start(out=gain_row[0:1, :], in_=k_norm_w.unsqueeze(0))
         down_scales_i32 = w_kv_down_scales.bitcast(I32)
         for quad in range(4):
             nc.sync.dma_start(
@@ -120,16 +120,6 @@ def tile_mla_pa_t_kernel(
         )
         for s in range(1, GROUP_TILES):
             nc.sync.dma_start(out=x_sb[0][:, s, :], in_=x_groups[0, :, s, :])
-        nc.sync.dma_start(out=x_sb[1][:], in_=x_groups[1])
-        table_view = "(a p s) j -> p a s j"
-        nc.sync.dma_start(
-            out=cos_sb[:].rearrange("p (a s) j -> p a s j", s=GROUP_TILES),
-            in_=freqs_cos.rearrange(table_view, p=P, s=GROUP_TILES),
-        )
-        nc.sync.dma_start(
-            out=sin_sb[:].rearrange("p (a s) j -> p a s j", s=GROUP_TILES),
-            in_=freqs_sin.rearrange(table_view, p=P, s=GROUP_TILES),
-        )
         up_scales_i32 = w_kv_up_scales.bitcast(I32)
         for quad in range(4):
             nc.sync.dma_start(
@@ -140,8 +130,20 @@ def tile_mla_pa_t_kernel(
             out=w_up[:].bitcast(I32),
             in_=w_kv_up_words[0].rearrange("p n t -> p (n t)").bitcast(I32),
         )
+        for s in range(GROUP_TILES):
+            nc.sync.dma_start(out=x_sb[1][:, s, :], in_=x_groups[1, :, s, :])
         for g in range(2, N_GROUPS):
             nc.sync.dma_start(out=x_sb[g][:], in_=x_groups[g])
+        nc.gpsimd.dma_start(out=gain_row[0:1, :], in_=k_norm_w.unsqueeze(0))
+        table_view = "(a p s) j -> p a s j"
+        nc.gpsimd.dma_start(
+            out=cos_sb[:].rearrange("p (a s) j -> p a s j", s=GROUP_TILES),
+            in_=freqs_cos.rearrange(table_view, p=P, s=GROUP_TILES),
+        )
+        nc.gpsimd.dma_start(
+            out=sin_sb[:].rearrange("p (a s) j -> p a s j", s=GROUP_TILES),
+            in_=freqs_sin.rearrange(table_view, p=P, s=GROUP_TILES),
+        )
 
         w_down_sorted = const.tile([P, DOWN_PASSES, PACK, P], I32, name="w_down_sorted", align_bytes=64)
         planes_sorted = const.tile([P, DOWN_PASSES, PACK, P], U8, name="planes_sorted", align_bytes=64)
@@ -154,32 +156,34 @@ def tile_mla_pa_t_kernel(
             in_=w_down[:].bitcast(I32).rearrange("p g (m t) -> p g t m", t=PACK),
         )
 
-        gain_psum = psum_latt.tile([P, PACK, P], F32, name="latt")
-        nc.tensor.matmul(out=gain_psum[:, 0, :], lhsT=ones[:], rhs=gain_row[:], start=True, stop=True)
-        gain = const.tile([P, PAIRS, 2], F32, name="gain")
-        nc.vector.tensor_copy(out=gain[:].rearrange("p j e -> p (j e)"), in_=gain_psum[:, 0, :])
-
-        gain_signed = const.tile([P, PAIRS, 2], F32, name="gain_signed")
-        nc.gpsimd.tensor_copy(out=gain_signed[:, :, 0], in_=gain[:, :, 0])
-        nc.gpsimd.tensor_scalar(
-            out=gain_signed[:, :, 1], in0=gain[:, :, 1], scalar1=-1.0, scalar2=0.0, op0=MULT, op1=ADD
-        )
         table = const.tile([P, SEQ_TILES, 2, PAIRS, 2], F32, name="table")
-        for a in range(0, SEQ_TILES, GROUP_TILES):
-            tiles = slice(a, a + GROUP_TILES)
-            shape = [P, GROUP_TILES, PAIRS, 2]
-            nc.gpsimd.tensor_tensor(
-                out=table[:, tiles, 0],
-                in0=cos_sb[:, tiles, :].unsqueeze(3).to_broadcast(shape),
-                in1=gain[:].unsqueeze(1).to_broadcast(shape),
-                op=MULT,
+
+        def build_tables():
+            gain_psum = psum_v.tile([P, H * D], F32, name="v")
+            nc.tensor.matmul(out=gain_psum[:, 0:D], lhsT=ones[:], rhs=gain_row[:], start=True, stop=True)
+            gain = const.tile([P, PAIRS, 2], F32, name="gain")
+            nc.vector.tensor_copy(out=gain[:].rearrange("p j e -> p (j e)"), in_=gain_psum[:, 0:D])
+
+            gain_signed = const.tile([P, PAIRS, 2], F32, name="gain_signed")
+            nc.gpsimd.tensor_copy(out=gain_signed[:, :, 0], in_=gain[:, :, 0])
+            nc.gpsimd.tensor_scalar(
+                out=gain_signed[:, :, 1], in0=gain[:, :, 1], scalar1=-1.0, scalar2=0.0, op0=MULT, op1=ADD
             )
-            nc.gpsimd.tensor_tensor(
-                out=table[:, tiles, 1],
-                in0=sin_sb[:, tiles, :].unsqueeze(3).to_broadcast(shape),
-                in1=gain_signed[:].unsqueeze(1).to_broadcast(shape),
-                op=MULT,
-            )
+            for a in range(0, SEQ_TILES, GROUP_TILES):
+                tiles = slice(a, a + GROUP_TILES)
+                shape = [P, GROUP_TILES, PAIRS, 2]
+                nc.gpsimd.tensor_tensor(
+                    out=table[:, tiles, 0],
+                    in0=cos_sb[:, tiles, :].unsqueeze(3).to_broadcast(shape),
+                    in1=gain[:].unsqueeze(1).to_broadcast(shape),
+                    op=MULT,
+                )
+                nc.gpsimd.tensor_tensor(
+                    out=table[:, tiles, 1],
+                    in0=sin_sb[:, tiles, :].unsqueeze(3).to_broadcast(shape),
+                    in1=gain_signed[:].unsqueeze(1).to_broadcast(shape),
+                    op=MULT,
+                )
 
         xt_psum, x_grouped, x_codes, x_scales = {}, {}, {}, {}
         latt_psum, lat_grouped, lat_codes, lat_scales = {}, {}, {}, {}
@@ -187,7 +191,10 @@ def tile_mla_pa_t_kernel(
 
         def transpose_x(i):
             words = x_sb[i // GROUP_TILES][:, i % GROUP_TILES, :].bitcast(F32)
-            xt_psum[i] = psum_xt.tile([P, DOWN_PASSES, 2, P], F32, name="xt")
+            if 2 <= i < HEAD:
+                xt_psum[i] = psum_k.tile([P, DOWN_PASSES, 2, P], F32, name="k")
+            else:
+                xt_psum[i] = psum_xt.tile([P, DOWN_PASSES, 2, P], F32, name="xt")
             for g in range(DOWN_PASSES):
                 for u in range(2):
                     nc.tensor.transpose(
@@ -213,7 +220,10 @@ def tile_mla_pa_t_kernel(
             )
 
         def down_matmul(i):
-            latt_psum[i] = psum_latt.tile([P, PACK, P], F32, name="latt")
+            if 2 <= i < HEAD:
+                latt_psum[i] = psum_v.tile([P, PACK, P], F32, name="v")
+            else:
+                latt_psum[i] = psum_latt.tile([P, PACK, P], F32, name="latt")
             for t in range(PACK):
                 for g in range(DOWN_PASSES):
                     tokens = slice(g * P, (g + 1) * P)
@@ -338,21 +348,36 @@ def tile_mla_pa_t_kernel(
             if 0 <= i < N_TILES:
                 stage(i)
 
-        for r in range(-X_LEAD, N_TILES + 1):
-            run(regroup_latent, r + 2)
+        def catch_up(stage, made, upto, source):
+            for i in range(len(made), min(len(made) + 2, upto + 1, N_TILES)):
+                if source is None or i in source:
+                    stage(i)
+
+        for i in range(HEAD):
+            transpose_x(i)
+            if i < len(WARM_BEHIND_TILE):
+                keep_warm(WARM_BEHIND_TILE[i])
+            regroup_x(i)
+            quantise_x(i)
+        build_tables()
+        for i in range(HEAD):
+            down_matmul(i)
+            regroup_latent(i)
+            quantise_latent(i)
+
+        for r in range(0, N_TILES + 1):
+            catch_up(regroup_latent, lat_grouped, r + 2, latt_psum)
             run(up_matmul, r)
-            run(transpose_x, r + X_LEAD)
-            if r + X_LEAD < len(WARM_BEHIND_TILE):
-                keep_warm(WARM_BEHIND_TILE[r + X_LEAD])
-            run(down_matmul, r + 4)
+            catch_up(transpose_x, xt_psum, r + X_LEAD, None)
+            catch_up(down_matmul, latt_psum, r + 4, x_codes)
             run(sum_squares, r)
             if r < FIRST_SPARE:
                 run(copy_v, r)
                 run(inverse_rms, r)
-                run(regroup_x, r + X_LEAD)
+                catch_up(regroup_x, x_grouped, r + X_LEAD, xt_psum)
             else:
                 run(copy_v_round_rstd, r)
             run(rotate_k, r - 1)
-            run(quantise_x, r + 5)
-            run(quantise_latent, r + 2)
+            catch_up(quantise_x, x_codes, r + 5, x_grouped)
+            catch_up(quantise_latent, lat_codes, r + 2, lat_grouped)
             run(add_products, r - 1)

from contextlib import ExitStack

import concourse.masks as masks
import concourse.mybir as mybir

F32 = mybir.dt.float32
BF16 = mybir.dt.bfloat16
I32 = mybir.dt.int32
U32 = mybir.dt.uint32
U8 = mybir.dt.uint8
FP8X4 = mybir.dt.float8_e4m3fn_x4
MULT = mybir.AluOpType.mult
ADD = mybir.AluOpType.add
SQUARE = mybir.ActivationFunctionType.Square
RSQRT = mybir.ActivationFunctionType.Abs_reciprocal_sqrt

P = 128
PACK = 4
TOKENS = 4 * 1024
SEQ = 1024
C = 1024
R = 512
H = 4
D = 128
PAIRS = D // 2
EPS = 1e-6

DOWN_PASSES = C // (P * PACK)
GROUP_TILES = 4
N_TILES = TOKENS // P
N_GROUPS = N_TILES // GROUP_TILES
SEQ_TILES = SEQ // P
X_LEAD = 6
WARM_BEHIND_TILE = (3, 1)
HEAD = 4
FIRST_SPARE = N_TILES - X_LEAD

FLOPS = 2 * TOKENS * (C * R + R * 2 * H * D)


def tile_mla_pa_t_kernel(
    tc,
    x,
    w_kv_down_words,
    w_kv_down_scales,
    w_kv_up_words,
    w_kv_up_scales,
    k_norm_w,
    freqs_cos,
    freqs_sin,
    out_0,
    out_1,
):
    nc = tc.nc

    x_groups = x.flatten_outer_dims().rearrange("(g p s) c -> g p s c", p=P, s=GROUP_TILES)
    k_groups = out_0.rearrange("b t h d -> (b t) (h d)").rearrange(
        "(g p s) n -> g p s n", p=P, s=GROUP_TILES
    )
    v_groups = out_1.rearrange("b t h d -> (b t) (h d)").rearrange(
        "(g p s) n -> g p s n", p=P, s=GROUP_TILES
    )

    with ExitStack() as ctx:
        ctx.enter_context(tc.manual_schedule())
        const = ctx.enter_context(tc.tile_pool(name="const", bufs=1))
        work = ctx.enter_context(tc.tile_pool(name="work", bufs=2))
        kept = ctx.enter_context(tc.tile_pool(name="kept", bufs=4))
        outs = ctx.enter_context(tc.tile_pool(name="outs", bufs=8))
        psum_xt = ctx.enter_context(tc.psum_pool(name="psum_xt", bufs=2))
        psum_latt = ctx.enter_context(tc.psum_pool(name="psum_latt", bufs=2))
        psum_k = ctx.enter_context(tc.psum_pool(name="psum_k", bufs=2))
        psum_v = ctx.enter_context(tc.psum_pool(name="psum_v", bufs=2))

        planes = const.tile([P, DOWN_PASSES * R + 2 * H * D], U8, name="planes", align_bytes=64)
        planes_i32 = planes[:].bitcast(I32)
        nc.vector.memset(planes_i32, 0)
        eps_col = const.tile([P, 1], F32, name="eps_col")
        nc.vector.memset(eps_col[:], EPS)

        ident_f32 = const.tile([P, P], F32, name="ident_f32")
        masks.make_identity(nc, ident_f32[:])

        warm = const.tile([P, 1], F32, name="warm")
        nc.scalar.activation(out=warm[:], in_=eps_col[:], func=RSQRT)

        gain_row = const.tile([P, D], BF16, name="gain_row")
        nc.vector.memset(gain_row[:], 0.0)
        ones = const.tile([P, P], BF16, name="ones")
        nc.vector.memset(ones[:], 1.0)
        zeros = const.tile([P, H * D], BF16, name="zeros")
        nc.vector.memset(zeros[:], 0.0)

        def keep_warm(count):
            bank = psum_v.tile([P, H * D], F32, name="v")
            for n in range(count):
                nc.tensor.matmul(out=bank[:], lhsT=ones[:], rhs=zeros[:], start=True, stop=True)

        keep_warm(4)
        cos_sb = const.tile([P, SEQ_TILES, PAIRS], BF16, name="cos_sb")
        sin_sb = const.tile([P, SEQ_TILES, PAIRS], BF16, name="sin_sb")
        x_sb = [const.tile([P, GROUP_TILES, C], BF16, name="x%d" % g) for g in range(N_GROUPS)]
        w_down = const.tile([P, DOWN_PASSES, R * PACK], U8, name="w_down", align_bytes=64)
        w_up = const.tile([P, 2 * H * D * PACK], U8, name="w_up", align_bytes=64)

        nc.sync.dma_start(out=x_sb[0][:, 0, :], in_=x_groups[0, :, 0, :])
        down_scales_i32 = w_kv_down_scales.bitcast(I32)
        for quad in range(4):
            nc.sync.dma_start(
                out=planes_i32[32 * quad : 32 * quad + 4, 0 : DOWN_PASSES * R // 4].rearrange(
                    "r (g n) -> r g n", g=DOWN_PASSES
                ),
                in_=down_scales_i32[:, 4 * quad : 4 * quad + 4, :].rearrange("g r n -> r g n"),
            )
        nc.sync.dma_start(
            out=w_down[:].bitcast(I32),
            in_=w_kv_down_words.rearrange("g p n t -> g p (n t)")
            .bitcast(I32)
            .rearrange("g p n -> p g n"),
        )
        for s in range(1, GROUP_TILES):
            nc.sync.dma_start(out=x_sb[0][:, s, :], in_=x_groups[0, :, s, :])
        up_scales_i32 = w_kv_up_scales.bitcast(I32)
        for quad in range(4):
            nc.sync.dma_start(
                out=planes_i32[32 * quad : 32 * quad + 4, DOWN_PASSES * R // 4 :],
                in_=up_scales_i32[0, 4 * quad : 4 * quad + 4, :],
            )
        nc.sync.dma_start(
            out=w_up[:].bitcast(I32),
            in_=w_kv_up_words[0].rearrange("p n t -> p (n t)").bitcast(I32),
        )
        for s in range(GROUP_TILES):
            nc.sync.dma_start(out=x_sb[1][:, s, :], in_=x_groups[1, :, s, :])
        for g in range(2, N_GROUPS):
            nc.sync.dma_start(out=x_sb[g][:], in_=x_groups[g])
        nc.gpsimd.dma_start(out=gain_row[0:1, :], in_=k_norm_w.unsqueeze(0))
        table_view = "(a p s) j -> p a s j"
        nc.gpsimd.dma_start(
            out=cos_sb[:].rearrange("p (a s) j -> p a s j", s=GROUP_TILES),
            in_=freqs_cos.rearrange(table_view, p=P, s=GROUP_TILES),
        )
        nc.gpsimd.dma_start(
            out=sin_sb[:].rearrange("p (a s) j -> p a s j", s=GROUP_TILES),
            in_=freqs_sin.rearrange(table_view, p=P, s=GROUP_TILES),
        )

        w_down_sorted = const.tile([P, DOWN_PASSES, PACK, P], I32, name="w_down_sorted", align_bytes=64)
        planes_sorted = const.tile([P, DOWN_PASSES, PACK, P], U8, name="planes_sorted", align_bytes=64)
        nc.vector.tensor_copy(
            out=planes_sorted[:],
            in_=planes[:, 0 : DOWN_PASSES * R].rearrange("p (g m t) -> p g t m", g=DOWN_PASSES, t=PACK),
        )
        nc.vector.tensor_copy(
            out=w_down_sorted[:],
            in_=w_down[:].bitcast(I32).rearrange("p g (m t) -> p g t m", t=PACK),
        )

        table = const.tile([P, SEQ_TILES, 2, PAIRS, 2], F32, name="table")

        def build_tables():
            gain_psum = psum_v.tile([P, H * D], F32, name="v")
            nc.tensor.matmul(out=gain_psum[:, 0:D], lhsT=ones[:], rhs=gain_row[:], start=True, stop=True)
            gain = const.tile([P, PAIRS, 2], F32, name="gain")
            nc.vector.tensor_copy(out=gain[:].rearrange("p j e -> p (j e)"), in_=gain_psum[:, 0:D])

            gain_signed = const.tile([P, PAIRS, 2], F32, name="gain_signed")
            nc.gpsimd.tensor_copy(out=gain_signed[:, :, 0], in_=gain[:, :, 0])
            nc.gpsimd.tensor_scalar(
                out=gain_signed[:, :, 1], in0=gain[:, :, 1], scalar1=-1.0, scalar2=0.0, op0=MULT, op1=ADD
            )
            for a in range(0, SEQ_TILES, GROUP_TILES):
                tiles = slice(a, a + GROUP_TILES)
                shape = [P, GROUP_TILES, PAIRS, 2]
                nc.gpsimd.tensor_tensor(
                    out=table[:, tiles, 0],
                    in0=cos_sb[:, tiles, :].unsqueeze(3).to_broadcast(shape),
                    in1=gain[:].unsqueeze(1).to_broadcast(shape),
                    op=MULT,
                )
                nc.gpsimd.tensor_tensor(
                    out=table[:, tiles, 1],
                    in0=sin_sb[:, tiles, :].unsqueeze(3).to_broadcast(shape),
                    in1=gain_signed[:].unsqueeze(1).to_broadcast(shape),
                    op=MULT,
                )

        xt_psum, x_grouped, x_codes, x_scales = {}, {}, {}, {}
        latt_psum, lat_grouped, lat_codes, lat_scales = {}, {}, {}, {}
        k_psum, v_psum, sums, rstd, products = {}, {}, {}, {}, {}

        def transpose_x(i):
            words = x_sb[i // GROUP_TILES][:, i % GROUP_TILES, :].bitcast(F32)
            if 2 <= i < HEAD:
                xt_psum[i] = psum_k.tile([P, DOWN_PASSES, 2, P], F32, name="k")
            else:
                xt_psum[i] = psum_xt.tile([P, DOWN_PASSES, 2, P], F32, name="xt")
            for g in range(DOWN_PASSES):
                for u in range(2):
                    nc.tensor.transpose(
                        xt_psum[i][:, g, u, :],
                        words[:, 2 * P * g + u : 2 * P * (g + 1) : 2],
                        ident_f32[:],
                    )

        def regroup_x(i):
            x_grouped[i] = work.tile([P, DOWN_PASSES, P, PACK], BF16, name="xg", align_bytes=64)
            nc.scalar.copy(
                out=x_grouped[i][:].bitcast(F32),
                in_=xt_psum[i][:].rearrange("p g u m -> p g m u"),
            )

        def quantise_x(i):
            x_codes[i] = kept.tile([P, DOWN_PASSES * P], U32, name="xq", align_bytes=64)
            x_scales[i] = kept.tile([P, DOWN_PASSES * P], U8, name="xs", align_bytes=64)
            nc.vector.quantize_mx(
                out=x_codes[i][:].bitcast(FP8X4),
                scales=x_scales[i][:],
                in_=x_grouped[i][:].rearrange("p g m t -> p (g m t)"),
            )

        def down_matmul(i):
            if 2 <= i < HEAD:
                latt_psum[i] = psum_v.tile([P, PACK, P], F32, name="v")
            else:
                latt_psum[i] = psum_latt.tile([P, PACK, P], F32, name="latt")
            for t in range(PACK):
                for g in range(DOWN_PASSES):
                    tokens = slice(g * P, (g + 1) * P)
                    nc.tensor.matmul_mx(
                        out=latt_psum[i][:, t, :],
                        lhsT=w_down_sorted[:, g, t, :].bitcast(FP8X4),
                        lhsT_scale=planes_sorted[:, g, t, :],
                        rhs=x_codes[i][:, tokens].bitcast(FP8X4),
                        rhs_scale=x_scales[i][:, tokens],
                        start=(g == 0),
                        stop=(g == DOWN_PASSES - 1),
                    )

        def on_scalar(i):
            return i % 3 == 2

        def regroup_latent(i):
            lat_grouped[i] = work.tile([P, P, PACK], BF16, name="lg", align_bytes=64)
            if on_scalar(i):
                nc.scalar.copy(out=lat_grouped[i][:], in_=latt_psum[i][:].rearrange("p t m -> p m t"))
            else:
                nc.vector.tensor_copy(
                    out=lat_grouped[i][:], in_=latt_psum[i][:].rearrange("p t m -> p m t")
                )

        def quantise_latent(i):
            lat_codes[i] = kept.tile([P, P], U32, name="lq", align_bytes=64)
            lat_scales[i] = kept.tile([P, P], U8, name="lsc", align_bytes=64)
            nc.vector.quantize_mx(
                out=lat_codes[i][:].bitcast(FP8X4),
                scales=lat_scales[i][:],
                in_=lat_grouped[i][:].rearrange("p m t -> p (m t)"),
            )

        def up_matmul(i):
            if i >= FIRST_SPARE and (i - FIRST_SPARE) % 4 < 2:
                k_psum[i] = psum_xt.tile([P, H * D], F32, name="xt")
            else:
                k_psum[i] = psum_k.tile([P, H * D], F32, name="k")
            v_psum[i] = psum_v.tile([P, H * D], F32, name="v")
            for half, bank in enumerate((k_psum[i], v_psum[i])):
                nc.tensor.matmul_mx(
                    out=bank[:],
                    lhsT=lat_codes[i][:].bitcast(FP8X4),
                    lhsT_scale=lat_scales[i][:],
                    rhs=w_up[:, half * H * D * PACK : (half + 1) * H * D * PACK].bitcast(FP8X4),
                    rhs_scale=planes[
                        :, DOWN_PASSES * R + half * H * D : DOWN_PASSES * R + (half + 1) * H * D
                    ],
                    start=True,
                    stop=True,
                )

        def sum_squares(i):
            squares = work.tile([P, H, D], BF16, name="squares")
            sums[i] = work.tile([P, H], F32, name="sums")
            for h in range(H):
                nc.scalar.activation(
                    out=squares[:, h, :],
                    in_=k_psum[i][:, h * D : (h + 1) * D],
                    func=SQUARE,
                    accum_out=sums[i][:, h : h + 1],
                )

        def inverse_rms(i):
            rstd[i] = kept.tile([P, H], F32, name="rstd")
            nc.scalar.activation(
                out=rstd[i][:], in_=sums[i][:], func=RSQRT, scale=1.0 / D, bias=eps_col[:, 0:1]
            )

        def copy_v(i):
            v_out = outs.tile([P, H * D], F32, name="v_out")
            nc.scalar.copy(out=v_out[:], in_=v_psum[i][:])
            nc.sync.dma_start(out=v_groups[i // GROUP_TILES, :, i % GROUP_TILES, :], in_=v_out[:])

        def copy_v_round_rstd(i):
            half = H * D // 2
            v_out = outs.tile([P, H * D], F32, name="v_out")
            nc.scalar.copy(out=v_out[:, 0:half], in_=v_psum[i][:, 0:half])
            inverse_rms(i)
            nc.scalar.copy(out=v_out[:, half:], in_=v_psum[i][:, half:])
            nc.sync.dma_start(out=v_groups[i // GROUP_TILES, :, i % GROUP_TILES, :], in_=v_out[:])

        def rotate_k(i):
            products[i] = kept.tile([P, H, 2, D], F32, name="products")
            for h in range(H):
                nc.vector.scalar_tensor_tensor(
                    out=products[i][:, h],
                    in0=k_psum[i][:, h * D : (h + 1) * D].unsqueeze(1).to_broadcast([P, 2, D]),
                    scalar=rstd[i][:, h : h + 1],
                    in1=table[:, i % SEQ_TILES].rearrange("p w j e -> p w (j e)"),
                    op0=MULT,
                    op1=MULT,
                )

        def add_products(i):
            pairs = products[i][:].rearrange("m h w (j e) -> m h w j e", e=2)
            k_out = outs.tile([P, H, PAIRS, 2], F32, name="k_out")
            if i < N_TILES - 1:
                nc.gpsimd.tensor_tensor(
                    out=k_out[:], in0=pairs[:, :, 0, :, :], in1=pairs[:, :, 1, :, ::-1], op=ADD
                )
                nc.sync.dma_start(
                    out=k_groups[i // GROUP_TILES, :, i % GROUP_TILES, :],
                    in_=k_out[:].rearrange("m h j e -> m (h j e)"),
                )
                return
            for first in range(0, H, 2):
                heads = slice(first, first + 2)
                nc.vector.tensor_tensor(
                    out=k_out[:, heads],
                    in0=pairs[:, heads, 0, :, :],
                    in1=pairs[:, heads, 1, :, ::-1],
                    op=ADD,
                )
                nc.sync.dma_start(
                    out=k_groups[i // GROUP_TILES, :, i % GROUP_TILES, first * D : (first + 2) * D],
                    in_=k_out[:, heads].rearrange("m h j e -> m (h j e)"),
                )

        def run(stage, i):
            if 0 <= i < N_TILES:
                stage(i)

        def catch_up(stage, made, upto, source):
            for i in range(len(made), min(len(made) + 2, upto + 1, N_TILES)):
                if source is None or i in source:
                    stage(i)

        for i in range(HEAD):
            transpose_x(i)
            if i < len(WARM_BEHIND_TILE):
                keep_warm(WARM_BEHIND_TILE[i])
            regroup_x(i)
            quantise_x(i)
        build_tables()
        for i in range(HEAD):
            down_matmul(i)
            regroup_latent(i)
            quantise_latent(i)

        for r in range(0, N_TILES + 1):
            catch_up(regroup_latent, lat_grouped, r + 2, latt_psum)
            run(up_matmul, r)
            catch_up(transpose_x, xt_psum, r + X_LEAD, None)
            catch_up(down_matmul, latt_psum, r + 4, x_codes)
            run(sum_squares, r)
            if r < FIRST_SPARE:
                run(copy_v, r)
                run(inverse_rms, r)
                catch_up(regroup_x, x_grouped, r + X_LEAD, xt_psum)
            else:
                run(copy_v_round_rstd, r)
            run(rotate_k, r - 1)
            catch_up(quantise_x, x_codes, r + 5, x_grouped)
            catch_up(quantise_latent, lat_codes, r + 2, lat_grouped)
            run(add_products, r - 1)
